import numpy as np
import ml_dtypes

BF16 = ml_dtypes.bfloat16


def bf(x):
    return np.asarray(x, np.float32).astype(BF16)


def f32(x):
    return np.asarray(x, np.float32)


def f64(x):
    return np.asarray(x).astype(np.float64)


def striped(idx):
    return np.tile(idx.reshape(-1, 16).T, (8, 1))


C, S, N, HID = 256, 2048, 512, 512


def setup_inputs():
    return {'emb': f32(np.random.standard_normal((C, S))), 'nf': f32(np.random.standard_normal((C, N))), 'adj_t': bf(np.random.standard_normal((N, N)) / np.sqrt(N)), 'w1': bf(np.random.standard_normal((C, HID)) / np.sqrt(C)), 'b1': f32(0.1 * np.random.standard_normal((HID, 1))), 'offs': striped(np.random.permutation(S)[:N])}


def reference(emb, nf, adj_t, w1, b1, offs):
    idx = offs[:16].T.reshape(-1)
    x = f64(emb)[:, idx] * f64(nf)
    agg = x @ f64(adj_t)
    return np.maximum(f64(w1).T @ agg + f64(b1), 0.0)

@@ -1,0 +1,71 @@
+import concourse.mybir as mybir
+from concourse.masks import make_identity
+
+P = 128
+C, S, N, HID = 256, 2048, 512, 512
+CB, JB, HB = C // P, N // P, HID // P
+FLOPS = 2 * C * N * N + 2 * C * N * HID
+
+F32, BF16, U16 = mybir.dt.float32, mybir.dt.bfloat16, mybir.dt.uint16
+MULT, ADD, MAX = mybir.AluOpType.mult, mybir.AluOpType.add, mybir.AluOpType.max
+RELU = mybir.ActivationFunctionType.Relu
+
+
+def tile_gcn_rec_kernel(tc, emb, nf, adj_t, w1, b1, offs, out):
+    nc = tc.nc
+    with (
+        tc.tile_pool(name="held", bufs=1) as held,
+        tc.tile_pool(name="stage", bufs=2) as stage,
+        tc.psum_pool(name="flip", bufs=2) as flip,
+        tc.psum_pool(name="sums", bufs=2) as sums,
+        tc.psum_pool(name="outs", bufs=1) as outs,
+    ):
+        offsets = held.tile([P, N // 16], U16, name="offsets")
+        nc.sync.dma_start(offsets[:], offs)
+        emb_sb = [held.tile([P, S], F32, name=f"emb{b}") for b in range(CB)]
+        nf_sb = [held.tile([P, N], F32, name=f"nf{b}") for b in range(CB)]
+        adj_sb = held.tile([P, JB, N], BF16, name="adj_sb")
+        w1_sb = held.tile([P, CB, HID], BF16, name="w1_sb")
+        b1_sb = held.tile([P, HB], F32, name="b1_sb")
+        nc.sync.dma_start(emb_sb[0][:], emb[0:P, :])
+        nc.sync.dma_start(nf_sb[0][:], nf[0:P, :])
+        nc.sync.dma_start(adj_sb[:], adj_t.rearrange("(t p) i -> p t i", p=P))
+        nc.sync.dma_start(emb_sb[1][:], emb[P : 2 * P, :])
+        nc.sync.dma_start(nf_sb[1][:], nf[P : 2 * P, :])
+        nc.sync.dma_start(w1_sb[:], w1.rearrange("(b p) h -> p b h", p=P))
+        with nc.allow_non_contiguous_dma(reason="512 bias values, one to a partition"):
+            nc.scalar.dma_start(b1_sb[:], b1.rearrange("(k p) o -> p (k o)", p=P))
+
+        identity = held.tile([P, P], F32, name="identity")
+        make_identity(nc, identity[:])
+
+        out_ps = [outs.tile([P, N], F32, name=f"out_ps{k}") for k in range(HB)]
+
+        for b in range(CB):
+            x = stage.tile([P, N], F32, name="x")
+            nc.vector.tensor_tensor(x[:], emb_sb[b][:].indirect(offsets[:]), nf_sb[b][:], MULT)
+
+            xT_ps = flip.tile([P, JB, P], F32, name="xT_ps")
+            for t in range(JB):
+                nc.tensor.transpose(xT_ps[:, t, :], x[:, t * P : (t + 1) * P], identity[:])
+            xT = stage.tile([P, JB, P], BF16, name="xT")
+            nc.scalar.copy(xT[:], xT_ps[:])
+
+            agg_ps = sums.tile([P, N], F32, name="agg_ps")
+            for t in range(JB):
+                nc.tensor.matmul(agg_ps[:], xT[:, t, :], adj_sb[:, t, :], start=(t == 0), stop=(t == JB - 1))
+            agg = stage.tile([P, N], BF16, name="agg")
+            nc.vector.tensor_copy(agg[:], agg_ps[:])
+
+            for k in range(HB):
+                nc.tensor.matmul(
+                    out_ps[k][:], w1_sb[:, b, k * P : (k + 1) * P], agg[:], start=(b == 0), stop=(b == CB - 1)
+                )
+
+        for k in range(HB):
+            y = stage.tile([P, N], F32, name="y")
+            if k % 2 == 0:
+                nc.scalar.activation(y[:], out_ps[k][:], RELU, bias=b1_sb[:, k : k + 1])
+            else:
+                nc.vector.tensor_scalar(y[:], out_ps[k][:], b1_sb[:, k : k + 1], 0.0, op0=ADD, op1=MAX)
+            nc.sync.dma_start(out[k * P : (k + 1) * P, :], y[:])

@@ -15,9 +15,8 @@ def tile_gcn_rec_kernel(tc, emb, nf, adj_t, w1, b1, offs, out):
     nc = tc.nc
     with (
         tc.tile_pool(name="held", bufs=1) as held,
-        tc.tile_pool(name="stage", bufs=2) as stage,
         tc.psum_pool(name="flip", bufs=2) as flip,
-        tc.psum_pool(name="sums", bufs=2) as sums,
+        tc.psum_pool(name="sums", bufs=1) as sums,
         tc.psum_pool(name="outs", bufs=1) as outs,
     ):
         offsets = held.tile([P, N // 16], U16, name="offsets")
@@ -27,11 +26,11 @@ def tile_gcn_rec_kernel(tc, emb, nf, adj_t, w1, b1, offs, out):
         adj_sb = held.tile([P, JB, N], BF16, name="adj_sb")
         w1_sb = held.tile([P, CB, HID], BF16, name="w1_sb")
         b1_sb = held.tile([P, HB], F32, name="b1_sb")
-        nc.sync.dma_start(emb_sb[0][:], emb[0:P, :])
-        nc.sync.dma_start(nf_sb[0][:], nf[0:P, :])
-        nc.sync.dma_start(adj_sb[:], adj_t.rearrange("(t p) i -> p t i", p=P))
-        nc.sync.dma_start(emb_sb[1][:], emb[P : 2 * P, :])
-        nc.sync.dma_start(nf_sb[1][:], nf[P : 2 * P, :])
+        for b in range(CB):
+            nc.sync.dma_start(emb_sb[b][:], emb[b * P : (b + 1) * P, :])
+            nc.sync.dma_start(nf_sb[b][:], nf[b * P : (b + 1) * P, :])
+        for t in range(JB):
+            nc.sync.dma_start(adj_sb[:, t, :], adj_t[t * P : (t + 1) * P, :])
         nc.sync.dma_start(w1_sb[:], w1.rearrange("(b p) h -> p b h", p=P))
         with nc.allow_non_contiguous_dma(reason="512 bias values, one to a partition"):
             nc.scalar.dma_start(b1_sb[:], b1.rearrange("(k p) o -> p (k o)", p=P))
@@ -41,29 +40,38 @@ def tile_gcn_rec_kernel(tc, emb, nf, adj_t, w1, b1, offs, out):
 
         out_ps = [outs.tile([P, N], F32, name=f"out_ps{k}") for k in range(HB)]
 
+        xT = [held.tile([P, JB, P], BF16, name=f"xT{b}") for b in range(CB)]
         for b in range(CB):
-            x = stage.tile([P, N], F32, name="x")
-            nc.vector.tensor_tensor(x[:], emb_sb[b][:].indirect(offsets[:]), nf_sb[b][:], MULT)
-
-            xT_ps = flip.tile([P, JB, P], F32, name="xT_ps")
+            x = held.tile([P, N], F32, name=f"x{b}")
             for t in range(JB):
-                nc.tensor.transpose(xT_ps[:, t, :], x[:, t * P : (t + 1) * P], identity[:])
-            xT = stage.tile([P, JB, P], BF16, name="xT")
-            nc.scalar.copy(xT[:], xT_ps[:])
+                piece = slice(t * P, (t + 1) * P)
+                nc.vector.tensor_tensor(
+                    x[:, piece],
+                    emb_sb[b][:].indirect(offsets[:, t * (P // 16) : (t + 1) * (P // 16)]),
+                    nf_sb[b][:, piece],
+                    MULT,
+                )
+                xT_ps = flip.tile([P, P], F32, name="xT_ps")
+                nc.tensor.transpose(xT_ps[:], x[:, piece], identity[:])
+                nc.scalar.copy(xT[b][:, t, :], xT_ps[:])
 
-            agg_ps = sums.tile([P, N], F32, name="agg_ps")
+        agg = [held.tile([P, N], BF16, name=f"agg{b}") for b in range(CB)]
+        for b in range(CB):
+            agg_ps = sums.tile([P, N], F32, name=f"agg_ps{b}")
             for t in range(JB):
-                nc.tensor.matmul(agg_ps[:], xT[:, t, :], adj_sb[:, t, :], start=(t == 0), stop=(t == JB - 1))
-            agg = stage.tile([P, N], BF16, name="agg")
-            nc.vector.tensor_copy(agg[:], agg_ps[:])
+                nc.tensor.matmul(agg_ps[:], xT[b][:, t, :], adj_sb[:, t, :], start=(t == 0), stop=(t == JB - 1))
+            if b == 0:
+                nc.scalar.copy(agg[b][:], agg_ps[:])
+            else:
+                nc.vector.tensor_copy(agg[b][:], agg_ps[:])
 
+        for b in range(CB):
             for k in range(HB):
                 nc.tensor.matmul(
-                    out_ps[k][:], w1_sb[:, b, k * P : (k + 1) * P], agg[:], start=(b == 0), stop=(b == CB - 1)
+                    out_ps[k][:], w1_sb[:, b, k * P : (k + 1) * P], agg[b][:], start=(b == 0), stop=(b == CB - 1)
                 )
-
         for k in range(HB):
-            y = stage.tile([P, N], F32, name="y")
+            y = held.tile([P, N], F32, name=f"y{k}")
             if k % 2 == 0:
                 nc.scalar.activation(y[:], out_ps[k][:], RELU, bias=b1_sb[:, k : k + 1])
             else:

@@ -9,6 +9,7 @@ FLOPS = 2 * C * N * N + 2 * C * N * HID
 F32, BF16, U16 = mybir.dt.float32, mybir.dt.bfloat16, mybir.dt.uint16
 MULT, ADD, MAX = mybir.AluOpType.mult, mybir.AluOpType.add, mybir.AluOpType.max
 RELU = mybir.ActivationFunctionType.Relu
+WARM_UP = 12
 
 
 def tile_gcn_rec_kernel(tc, emb, nf, adj_t, w1, b1, offs, out):
@@ -40,6 +41,11 @@ def tile_gcn_rec_kernel(tc, emb, nf, adj_t, w1, b1, offs, out):
 
         out_ps = [outs.tile([P, N], F32, name=f"out_ps{k}") for k in range(HB)]
 
+        zeros = held.tile([P, N], BF16, name="zeros")
+        nc.gpsimd.memset(zeros[:], 0.0)
+        for w in range(WARM_UP):
+            nc.tensor.matmul(out_ps[HB - 1][:], zeros[:, 0:P], zeros[:], start=True, stop=True)
+
         xT = [held.tile([P, JB, P], BF16, name=f"xT{b}") for b in range(CB)]
         for b in range(CB):
             x = held.tile([P, N], F32, name=f"x{b}")
@@ -54,6 +60,8 @@ def tile_gcn_rec_kernel(tc, emb, nf, adj_t, w1, b1, offs, out):
                 xT_ps = flip.tile([P, P], F32, name="xT_ps")
                 nc.tensor.transpose(xT_ps[:], x[:, piece], identity[:])
                 nc.scalar.copy(xT[b][:, t, :], xT_ps[:])
+                if b == 0:
+                    nc.tensor.matmul(out_ps[HB - 1][:], xT[b][:, t, :], zeros[:], start=True, stop=True)
 
         agg = [held.tile([P, N], BF16, name=f"agg{b}") for b in range(CB)]
         for b in range(CB):

@@ -9,7 +9,7 @@ FLOPS = 2 * C * N * N + 2 * C * N * HID
 F32, BF16, U16 = mybir.dt.float32, mybir.dt.bfloat16, mybir.dt.uint16
 MULT, ADD, MAX = mybir.AluOpType.mult, mybir.AluOpType.add, mybir.AluOpType.max
 RELU = mybir.ActivationFunctionType.Relu
-WARM_UP = 12
+WARM_UP = 16
 
 
 def tile_gcn_rec_kernel(tc, emb, nf, adj_t, w1, b1, offs, out):

@@ -9,7 +9,7 @@ FLOPS = 2 * C * N * N + 2 * C * N * HID
 F32, BF16, U16 = mybir.dt.float32, mybir.dt.bfloat16, mybir.dt.uint16
 MULT, ADD, MAX = mybir.AluOpType.mult, mybir.AluOpType.add, mybir.AluOpType.max
 RELU = mybir.ActivationFunctionType.Relu
-WARM_UP = 16
+WARM_UP = 12
 
 
 def tile_gcn_rec_kernel(tc, emb, nf, adj_t, w1, b1, offs, out):
@@ -34,7 +34,7 @@ def tile_gcn_rec_kernel(tc, emb, nf, adj_t, w1, b1, offs, out):
             nc.sync.dma_start(adj_sb[:, t, :], adj_t[t * P : (t + 1) * P, :])
         nc.sync.dma_start(w1_sb[:], w1.rearrange("(b p) h -> p b h", p=P))
         with nc.allow_non_contiguous_dma(reason="512 bias values, one to a partition"):
-            nc.scalar.dma_start(b1_sb[:], b1.rearrange("(k p) o -> p (k o)", p=P))
+            nc.sync.dma_start(b1_sb[:], b1.rearrange("(k p) o -> p (k o)", p=P))
 
         identity = held.tile([P, P], F32, name="identity")
         make_identity(nc, identity[:])

@@ -4,6 +4,8 @@ from concourse.masks import make_identity
 P = 128
 C, S, N, HID = 256, 2048, 512, 512
 CB, JB, HB = C // P, N // P, HID // P
+HALVES = 2
+W = N // HALVES
 FLOPS = 2 * C * N * N + 2 * C * N * HID
 
 F32, BF16, U16 = mybir.dt.float32, mybir.dt.bfloat16, mybir.dt.uint16
@@ -16,22 +18,21 @@ def tile_gcn_rec_kernel(tc, emb, nf, adj_t, w1, b1, offs, out):
     nc = tc.nc
     with (
         tc.tile_pool(name="held", bufs=1) as held,
-        tc.psum_pool(name="flip", bufs=2) as flip,
-        tc.psum_pool(name="sums", bufs=1) as sums,
-        tc.psum_pool(name="outs", bufs=1) as outs,
+        tc.psum_pool(name="banks", bufs=8) as banks,
     ):
         offsets = held.tile([P, N // 16], U16, name="offsets")
         nc.sync.dma_start(offsets[:], offs)
         emb_sb = [held.tile([P, S], F32, name=f"emb{b}") for b in range(CB)]
-        nf_sb = [held.tile([P, N], F32, name=f"nf{b}") for b in range(CB)]
-        adj_sb = held.tile([P, JB, N], BF16, name="adj_sb")
+        nf_sb = [[held.tile([P, P], F32, name=f"nf{b}_{t}") for t in range(JB)] for b in range(CB)]
+        adj_sb = [held.tile([P, N], BF16, name=f"adj{t}") for t in range(JB)]
         w1_sb = held.tile([P, CB, HID], BF16, name="w1_sb")
         b1_sb = held.tile([P, HB], F32, name="b1_sb")
         for b in range(CB):
             nc.sync.dma_start(emb_sb[b][:], emb[b * P : (b + 1) * P, :])
-            nc.sync.dma_start(nf_sb[b][:], nf[b * P : (b + 1) * P, :])
-        for t in range(JB):
-            nc.sync.dma_start(adj_sb[:, t, :], adj_t[t * P : (t + 1) * P, :])
+            for t in range(JB):
+                nc.sync.dma_start(nf_sb[b][t][:], nf[b * P : (b + 1) * P, t * P : (t + 1) * P])
+                if b == CB - 1:
+                    nc.sync.dma_start(adj_sb[t][:], adj_t[t * P : (t + 1) * P, :])
         nc.sync.dma_start(w1_sb[:], w1.rearrange("(b p) h -> p b h", p=P))
         with nc.allow_non_contiguous_dma(reason="512 bias values, one to a partition"):
             nc.sync.dma_start(b1_sb[:], b1.rearrange("(k p) o -> p (k o)", p=P))
@@ -39,14 +40,14 @@ def tile_gcn_rec_kernel(tc, emb, nf, adj_t, w1, b1, offs, out):
         identity = held.tile([P, P], F32, name="identity")
         make_identity(nc, identity[:])
 
-        out_ps = [outs.tile([P, N], F32, name=f"out_ps{k}") for k in range(HB)]
-
         zeros = held.tile([P, N], BF16, name="zeros")
         nc.gpsimd.memset(zeros[:], 0.0)
+        warm_ps = banks.tile([P, N], F32, name="warm_ps", tag="bank")
         for w in range(WARM_UP):
-            nc.tensor.matmul(out_ps[HB - 1][:], zeros[:, 0:P], zeros[:], start=True, stop=True)
+            nc.tensor.matmul(warm_ps[:], zeros[:, 0:P], zeros[:], start=True, stop=True)
 
         xT = [held.tile([P, JB, P], BF16, name=f"xT{b}") for b in range(CB)]
+        agg_ps = [banks.tile([P, N], F32, name=f"agg_ps{b}", tag="bank") for b in range(CB)]
         for b in range(CB):
             x = held.tile([P, N], F32, name=f"x{b}")
             for t in range(JB):
@@ -54,34 +55,39 @@ def tile_gcn_rec_kernel(tc, emb, nf, adj_t, w1, b1, offs, out):
                 nc.vector.tensor_tensor(
                     x[:, piece],
                     emb_sb[b][:].indirect(offsets[:, t * (P // 16) : (t + 1) * (P // 16)]),
-                    nf_sb[b][:, piece],
+                    nf_sb[b][t][:],
                     MULT,
                 )
-                xT_ps = flip.tile([P, P], F32, name="xT_ps")
-                nc.tensor.transpose(xT_ps[:], x[:, piece], identity[:])
-                nc.scalar.copy(xT[b][:, t, :], xT_ps[:])
+                xT_ps = banks.tile([P, P], F32, name="xT_ps", tag="bank")
                 if b == 0:
-                    nc.tensor.matmul(out_ps[HB - 1][:], xT[b][:, t, :], zeros[:], start=True, stop=True)
+                    nc.tensor.matmul(xT_ps[:], x[:, piece], identity[:], start=True, stop=True)
+                else:
+                    nc.tensor.transpose(xT_ps[:], x[:, piece], identity[:])
+                nc.scalar.copy(xT[b][:, t, :], xT_ps[:])
+                if b == CB - 1:
+                    nc.tensor.matmul(agg_ps[0][:], xT[0][:, t, :], adj_sb[t][:], start=(t == 0), stop=(t == JB - 1))
 
         agg = [held.tile([P, N], BF16, name=f"agg{b}") for b in range(CB)]
         for b in range(CB):
-            agg_ps = sums.tile([P, N], F32, name=f"agg_ps{b}")
-            for t in range(JB):
-                nc.tensor.matmul(agg_ps[:], xT[b][:, t, :], adj_sb[:, t, :], start=(t == 0), stop=(t == JB - 1))
-            if b == 0:
-                nc.scalar.copy(agg[b][:], agg_ps[:])
-            else:
-                nc.vector.tensor_copy(agg[b][:], agg_ps[:])
+            if b == CB - 1:
+                for t in range(JB):
+                    nc.tensor.matmul(agg_ps[b][:], xT[b][:, t, :], adj_sb[t][:], start=(t == 0), stop=(t == JB - 1))
+            nc.vector.tensor_copy(agg[b][:, 0:W], agg_ps[b][:, 0:W])
+            nc.scalar.copy(agg[b][:, W:N], agg_ps[b][:, W:N])
 
-        for b in range(CB):
+        y = [held.tile([P, N], F32, name=f"y{k}") for k in range(HB)]
+        for half in range(HALVES):
+            cols = slice(half * W, (half + 1) * W)
+            out_ps = [banks.tile([P, W], F32, name=f"out_ps{half}_{k}", tag="bank") for k in range(HB)]
+            for b in range(CB):
+                for k in range(HB):
+                    nc.tensor.matmul(
+                        out_ps[k][:], w1_sb[:, b, k * P : (k + 1) * P], agg[b][:, cols],
+                        start=(b == 0), stop=(b == CB - 1),
+                    )
             for k in range(HB):
-                nc.tensor.matmul(
-                    out_ps[k][:], w1_sb[:, b, k * P : (k + 1) * P], agg[b][:], start=(b == 0), stop=(b == CB - 1)
-                )
-        for k in range(HB):
-            y = held.tile([P, N], F32, name=f"y{k}")
-            if k % 2 == 0:
-                nc.scalar.activation(y[:], out_ps[k][:], RELU, bias=b1_sb[:, k : k + 1])
-            else:
-                nc.vector.tensor_scalar(y[:], out_ps[k][:], b1_sb[:, k : k + 1], 0.0, op0=ADD, op1=MAX)
-            nc.sync.dma_start(out[k * P : (k + 1) * P, :], y[:])
+                if k % 2 == 0:
+                    nc.scalar.activation(y[k][:, cols], out_ps[k][:], RELU, bias=b1_sb[:, k : k + 1])
+                else:
+                    nc.vector.tensor_scalar(y[k][:, cols], out_ps[k][:], b1_sb[:, k : k + 1], 0.0, op0=ADD, op1=MAX)
+                nc.sync.dma_start(out[k * P : (k + 1) * P, cols], y[k][:, cols])

@@ -4,8 +4,9 @@ from concourse.masks import make_identity
 P = 128
 C, S, N, HID = 256, 2048, 512, 512
 CB, JB, HB = C // P, N // P, HID // P
-HALVES = 2
-W = N // HALVES
+GB = 2
+G = N // GB
+TG = JB // GB
 FLOPS = 2 * C * N * N + 2 * C * N * HID
 
 F32, BF16, U16 = mybir.dt.float32, mybir.dt.bfloat16, mybir.dt.uint16
@@ -23,16 +24,18 @@ def tile_gcn_rec_kernel(tc, emb, nf, adj_t, w1, b1, offs, out):
         offsets = held.tile([P, N // 16], U16, name="offsets")
         nc.sync.dma_start(offsets[:], offs)
         emb_sb = [held.tile([P, S], F32, name=f"emb{b}") for b in range(CB)]
-        nf_sb = [[held.tile([P, P], F32, name=f"nf{b}_{t}") for t in range(JB)] for b in range(CB)]
-        adj_sb = [held.tile([P, N], BF16, name=f"adj{t}") for t in range(JB)]
+        nf_sb = [held.tile([P, N], F32, name=f"nf{b}") for b in range(CB)]
+        adj_sb = held.tile([P, JB, N], BF16, name="adj_sb")
         w1_sb = held.tile([P, CB, HID], BF16, name="w1_sb")
         b1_sb = held.tile([P, HB], F32, name="b1_sb")
-        for b in range(CB):
-            nc.sync.dma_start(emb_sb[b][:], emb[b * P : (b + 1) * P, :])
-            for t in range(JB):
-                nc.sync.dma_start(nf_sb[b][t][:], nf[b * P : (b + 1) * P, t * P : (t + 1) * P])
-                if b == CB - 1:
-                    nc.sync.dma_start(adj_sb[t][:], adj_t[t * P : (t + 1) * P, :])
+        nc.sync.dma_start(emb_sb[0][:], emb[0:P, :])
+        nc.sync.dma_start(nf_sb[0][:], nf[0:P, :])
+        nc.sync.dma_start(emb_sb[1][:], emb[P : 2 * P, :])
+        for g in range(GB):
+            nc.sync.dma_start(nf_sb[1][:, g * G : (g + 1) * G], nf[P : 2 * P, g * G : (g + 1) * G])
+            nc.sync.dma_start(
+                adj_sb[:, g * TG : (g + 1) * TG, :], adj_t[g * G : (g + 1) * G, :].rearrange("(t p) i -> p t i", p=P)
+            )
         nc.sync.dma_start(w1_sb[:], w1.rearrange("(b p) h -> p b h", p=P))
         with nc.allow_non_contiguous_dma(reason="512 bias values, one to a partition"):
             nc.sync.dma_start(b1_sb[:], b1.rearrange("(k p) o -> p (k o)", p=P))
@@ -50,44 +53,42 @@ def tile_gcn_rec_kernel(tc, emb, nf, adj_t, w1, b1, offs, out):
         agg_ps = [banks.tile([P, N], F32, name=f"agg_ps{b}", tag="bank") for b in range(CB)]
         for b in range(CB):
             x = held.tile([P, N], F32, name=f"x{b}")
-            for t in range(JB):
-                piece = slice(t * P, (t + 1) * P)
+            for g in range(GB):
                 nc.vector.tensor_tensor(
-                    x[:, piece],
-                    emb_sb[b][:].indirect(offsets[:, t * (P // 16) : (t + 1) * (P // 16)]),
-                    nf_sb[b][t][:],
+                    x[:, g * G : (g + 1) * G],
+                    emb_sb[b][:].indirect(offsets[:, g * (G // 16) : (g + 1) * (G // 16)]),
+                    nf_sb[b][:, g * G : (g + 1) * G],
                     MULT,
                 )
-                xT_ps = banks.tile([P, P], F32, name="xT_ps", tag="bank")
-                if b == 0:
-                    nc.tensor.matmul(xT_ps[:], x[:, piece], identity[:], start=True, stop=True)
-                else:
-                    nc.tensor.transpose(xT_ps[:], x[:, piece], identity[:])
-                nc.scalar.copy(xT[b][:, t, :], xT_ps[:])
-                if b == CB - 1:
-                    nc.tensor.matmul(agg_ps[0][:], xT[0][:, t, :], adj_sb[t][:], start=(t == 0), stop=(t == JB - 1))
+                for t in range(g * TG, (g + 1) * TG):
+                    xT_ps = banks.tile([P, P], F32, name="xT_ps", tag="bank")
+                    if b == 0:
+                        nc.tensor.matmul(xT_ps[:], x[:, t * P : (t + 1) * P], identity[:], start=True, stop=True)
+                    else:
+                        nc.tensor.transpose(xT_ps[:], x[:, t * P : (t + 1) * P], identity[:])
+                    nc.scalar.copy(xT[b][:, t, :], xT_ps[:])
+                if b == 1:
+                    for t in range(g * TG, (g + 1) * TG):
+                        nc.tensor.matmul(
+                            agg_ps[0][:], xT[0][:, t, :], adj_sb[:, t, :], start=(t == 0), stop=(t == JB - 1)
+                        )
+        for t in range(JB):
+            nc.tensor.matmul(agg_ps[1][:], xT[1][:, t, :], adj_sb[:, t, :], start=(t == 0), stop=(t == JB - 1))
 
         agg = [held.tile([P, N], BF16, name=f"agg{b}") for b in range(CB)]
         for b in range(CB):
-            if b == CB - 1:
-                for t in range(JB):
-                    nc.tensor.matmul(agg_ps[b][:], xT[b][:, t, :], adj_sb[t][:], start=(t == 0), stop=(t == JB - 1))
-            nc.vector.tensor_copy(agg[b][:, 0:W], agg_ps[b][:, 0:W])
-            nc.scalar.copy(agg[b][:, W:N], agg_ps[b][:, W:N])
+            nc.vector.tensor_copy(agg[b][:, 0 : N // 2], agg_ps[b][:, 0 : N // 2])
+            nc.scalar.copy(agg[b][:, N // 2 : N], agg_ps[b][:, N // 2 : N])
 
-        y = [held.tile([P, N], F32, name=f"y{k}") for k in range(HB)]
-        for half in range(HALVES):
-            cols = slice(half * W, (half + 1) * W)
-            out_ps = [banks.tile([P, W], F32, name=f"out_ps{half}_{k}", tag="bank") for k in range(HB)]
+        for k in range(HB):
+            out_ps = banks.tile([P, N], F32, name="out_ps", tag="bank")
             for b in range(CB):
-                for k in range(HB):
-                    nc.tensor.matmul(
-                        out_ps[k][:], w1_sb[:, b, k * P : (k + 1) * P], agg[b][:, cols],
-                        start=(b == 0), stop=(b == CB - 1),
-                    )
-            for k in range(HB):
-                if k % 2 == 0:
-                    nc.scalar.activation(y[k][:, cols], out_ps[k][:], RELU, bias=b1_sb[:, k : k + 1])
-                else:
-                    nc.vector.tensor_scalar(y[k][:, cols], out_ps[k][:], b1_sb[:, k : k + 1], 0.0, op0=ADD, op1=MAX)
-                nc.sync.dma_start(out[k * P : (k + 1) * P, cols], y[k][:, cols])
+                nc.tensor.matmul(
+                    out_ps[:], w1_sb[:, b, k * P : (k + 1) * P], agg[b][:], start=(b == 0), stop=(b == CB - 1)
+                )
+            y = held.tile([P, N], F32, name=f"y{k}")
+            if k % 2 == 0:
+                nc.scalar.activation(y[:], out_ps[:], RELU, bias=b1_sb[:, k : k + 1])
+            else:
+                nc.vector.tensor_scalar(y[:], out_ps[:], b1_sb[:, k : k + 1], 0.0, op0=ADD, op1=MAX)
+            nc.sync.dma_start(out[k * P : (k + 1) * P, :], y[:])

@@ -7,6 +7,8 @@ CB, JB, HB = C // P, N // P, HID // P
 GB = 2
 G = N // GB
 TG = JB // GB
+HALVES = 2
+W = N // HALVES
 FLOPS = 2 * C * N * N + 2 * C * N * HID
 
 F32, BF16, U16 = mybir.dt.float32, mybir.dt.bfloat16, mybir.dt.uint16
@@ -77,18 +79,22 @@ def tile_gcn_rec_kernel(tc, emb, nf, adj_t, w1, b1, offs, out):
 
         agg = [held.tile([P, N], BF16, name=f"agg{b}") for b in range(CB)]
         for b in range(CB):
-            nc.vector.tensor_copy(agg[b][:, 0 : N // 2], agg_ps[b][:, 0 : N // 2])
-            nc.scalar.copy(agg[b][:, N // 2 : N], agg_ps[b][:, N // 2 : N])
+            nc.vector.tensor_copy(agg[b][:, 0:W], agg_ps[b][:, 0:W])
+            nc.scalar.copy(agg[b][:, W:N], agg_ps[b][:, W:N])
 
-        for k in range(HB):
-            out_ps = banks.tile([P, N], F32, name="out_ps", tag="bank")
+        y = [held.tile([P, N], F32, name=f"y{k}") for k in range(HB)]
+        for half in range(HALVES):
+            cols = slice(half * W, (half + 1) * W)
+            out_ps = [banks.tile([P, W], F32, name=f"out_ps{half}_{k}", tag="bank") for k in range(HB)]
             for b in range(CB):
-                nc.tensor.matmul(
-                    out_ps[:], w1_sb[:, b, k * P : (k + 1) * P], agg[b][:], start=(b == 0), stop=(b == CB - 1)
-                )
-            y = held.tile([P, N], F32, name=f"y{k}")
-            if k % 2 == 0:
-                nc.scalar.activation(y[:], out_ps[:], RELU, bias=b1_sb[:, k : k + 1])
-            else:
-                nc.vector.tensor_scalar(y[:], out_ps[:], b1_sb[:, k : k + 1], 0.0, op0=ADD, op1=MAX)
-            nc.sync.dma_start(out[k * P : (k + 1) * P, :], y[:])
+                for k in range(HB):
+                    nc.tensor.matmul(
+                        out_ps[k][:], w1_sb[:, b, k * P : (k + 1) * P], agg[b][:, cols],
+                        start=(b == 0), stop=(b == CB - 1),
+                    )
+            for k in range(HB):
+                if k % 2 == 0:
+                    nc.scalar.activation(y[k][:, cols], out_ps[k][:], RELU, bias=b1_sb[:, k : k + 1])
+                else:
+                    nc.vector.tensor_scalar(y[k][:, cols], out_ps[k][:], b1_sb[:, k : k + 1], 0.0, op0=ADD, op1=MAX)
+                nc.sync.dma_start(out[k * P : (k + 1) * P, cols], y[k][:, cols])

@@ -14,7 +14,6 @@ FLOPS = 2 * C * N * N + 2 * C * N * HID
 F32, BF16, U16 = mybir.dt.float32, mybir.dt.bfloat16, mybir.dt.uint16
 MULT, ADD, MAX = mybir.AluOpType.mult, mybir.AluOpType.add, mybir.AluOpType.max
 RELU = mybir.ActivationFunctionType.Relu
-WARM_UP = 12
 
 
 def tile_gcn_rec_kernel(tc, emb, nf, adj_t, w1, b1, offs, out):
@@ -44,12 +43,6 @@ def tile_gcn_rec_kernel(tc, emb, nf, adj_t, w1, b1, offs, out):
 
         identity = held.tile([P, P], F32, name="identity")
         make_identity(nc, identity[:])
-
-        zeros = held.tile([P, N], BF16, name="zeros")
-        nc.gpsimd.memset(zeros[:], 0.0)
-        warm_ps = banks.tile([P, N], F32, name="warm_ps", tag="bank")
-        for w in range(WARM_UP):
-            nc.tensor.matmul(warm_ps[:], zeros[:, 0:P], zeros[:], start=True, stop=True)
 
         xT = [held.tile([P, JB, P], BF16, name=f"xT{b}") for b in range(CB)]
         agg_ps = [banks.tile([P, N], F32, name=f"agg_ps{b}", tag="bank") for b in range(CB)]

@@ -32,8 +32,8 @@ def tile_gcn_rec_kernel(tc, emb, nf, adj_t, w1, b1, offs, out):
         nc.sync.dma_start(emb_sb[0][:], emb[0:P, :])
         nc.sync.dma_start(nf_sb[0][:], nf[0:P, :])
         nc.sync.dma_start(emb_sb[1][:], emb[P : 2 * P, :])
+        nc.sync.dma_start(nf_sb[1][:], nf[P : 2 * P, :])
         for g in range(GB):
-            nc.sync.dma_start(nf_sb[1][:, g * G : (g + 1) * G], nf[P : 2 * P, g * G : (g + 1) * G])
             nc.sync.dma_start(
                 adj_sb[:, g * TG : (g + 1) * TG, :], adj_t[g * G : (g + 1) * G, :].rearrange("(t p) i -> p t i", p=P)
             )

@@ -45,35 +45,41 @@ def tile_gcn_rec_kernel(tc, emb, nf, adj_t, w1, b1, offs, out):
         make_identity(nc, identity[:])
 
         xT = [held.tile([P, JB, P], BF16, name=f"xT{b}") for b in range(CB)]
-        agg_ps = [banks.tile([P, N], F32, name=f"agg_ps{b}", tag="bank") for b in range(CB)]
+        agg_ps = [
+            [banks.tile([P, W], F32, name=f"agg_ps{b}_{half}", tag="bank") for half in range(HALVES)] for b in range(CB)
+        ]
+
+        def sum_over_j(b, t):
+            for half in range(HALVES):
+                nc.tensor.matmul(
+                    agg_ps[b][half][:], xT[b][:, t, :], adj_sb[:, t, half * W : (half + 1) * W],
+                    start=(t == 0), stop=(t == JB - 1),
+                )
+
         for b in range(CB):
             x = held.tile([P, N], F32, name=f"x{b}")
-            for g in range(GB):
+            for t in range(JB):
                 nc.vector.tensor_tensor(
-                    x[:, g * G : (g + 1) * G],
-                    emb_sb[b][:].indirect(offsets[:, g * (G // 16) : (g + 1) * (G // 16)]),
-                    nf_sb[b][:, g * G : (g + 1) * G],
+                    x[:, t * P : (t + 1) * P],
+                    emb_sb[b][:].indirect(offsets[:, t * (P // 16) : (t + 1) * (P // 16)]),
+                    nf_sb[b][:, t * P : (t + 1) * P],
                     MULT,
                 )
-                for t in range(g * TG, (g + 1) * TG):
-                    xT_ps = banks.tile([P, P], F32, name="xT_ps", tag="bank")
-                    if b == 0:
-                        nc.tensor.matmul(xT_ps[:], x[:, t * P : (t + 1) * P], identity[:], start=True, stop=True)
-                    else:
-                        nc.tensor.transpose(xT_ps[:], x[:, t * P : (t + 1) * P], identity[:])
-                    nc.scalar.copy(xT[b][:, t, :], xT_ps[:])
+                xT_ps = banks.tile([P, P], F32, name="xT_ps", tag="bank")
+                if b == 0:
+                    nc.tensor.matmul(xT_ps[:], x[:, t * P : (t + 1) * P], identity[:], start=True, stop=True)
+                else:
+                    nc.tensor.transpose(xT_ps[:], x[:, t * P : (t + 1) * P], identity[:])
+                nc.scalar.copy(xT[b][:, t, :], xT_ps[:])
                 if b == 1:
-                    for t in range(g * TG, (g + 1) * TG):
-                        nc.tensor.matmul(
-                            agg_ps[0][:], xT[0][:, t, :], adj_sb[:, t, :], start=(t == 0), stop=(t == JB - 1)
-                        )
+                    sum_over_j(0, t)
         for t in range(JB):
-            nc.tensor.matmul(agg_ps[1][:], xT[1][:, t, :], adj_sb[:, t, :], start=(t == 0), stop=(t == JB - 1))
+            sum_over_j(1, t)
 
         agg = [held.tile([P, N], BF16, name=f"agg{b}") for b in range(CB)]
         for b in range(CB):
-            nc.vector.tensor_copy(agg[b][:, 0:W], agg_ps[b][:, 0:W])
-            nc.scalar.copy(agg[b][:, W:N], agg_ps[b][:, W:N])
+            nc.vector.tensor_copy(agg[b][:, 0:W], agg_ps[b][0][:])
+            nc.scalar.copy(agg[b][:, W:N], agg_ps[b][1][:])
 
         y = [held.tile([P, N], F32, name=f"y{k}") for k in range(HB)]
         for half in range(HALVES):

@@ -32,7 +32,8 @@ def tile_gcn_rec_kernel(tc, emb, nf, adj_t, w1, b1, offs, out):
         nc.sync.dma_start(emb_sb[0][:], emb[0:P, :])
         nc.sync.dma_start(nf_sb[0][:], nf[0:P, :])
         nc.sync.dma_start(emb_sb[1][:], emb[P : 2 * P, :])
-        nc.sync.dma_start(nf_sb[1][:], nf[P : 2 * P, :])
+        for g in range(GB):
+            nc.sync.dma_start(nf_sb[1][:, g * G : (g + 1) * G], nf[P : 2 * P, g * G : (g + 1) * G])
         for g in range(GB):
             nc.sync.dma_start(
                 adj_sb[:, g * TG : (g + 1) * TG, :], adj_t[g * G : (g + 1) * G, :].rearrange("(t p) i -> p t i", p=P)

@@ -45,45 +45,44 @@ def tile_gcn_rec_kernel(tc, emb, nf, adj_t, w1, b1, offs, out):
         identity = held.tile([P, P], F32, name="identity")
         make_identity(nc, identity[:])
 
+        x = [held.tile([P, N], F32, name=f"x{b}") for b in range(CB)]
         xT = [held.tile([P, JB, P], BF16, name=f"xT{b}") for b in range(CB)]
+
+        def gate_and_flip(b, t):
+            piece = x[b][:, t * P : (t + 1) * P]
+            nc.vector.tensor_tensor(
+                piece,
+                emb_sb[b][:].indirect(offsets[:, t * (P // 16) : (t + 1) * (P // 16)]),
+                nf_sb[b][:, t * P : (t + 1) * P],
+                MULT,
+            )
+            xT_ps = banks.tile([P, P], F32, name="xT_ps", tag="bank")
+            if b == 0:
+                nc.tensor.matmul(xT_ps[:], piece, identity[:], start=True, stop=True)
+            else:
+                nc.tensor.transpose(xT_ps[:], piece, identity[:])
+            nc.scalar.copy(xT[b][:, t, :], xT_ps[:])
+
         agg_ps = [
             [banks.tile([P, W], F32, name=f"agg_ps{b}_{half}", tag="bank") for half in range(HALVES)] for b in range(CB)
         ]
-
-        def sum_over_j(b, t):
-            for half in range(HALVES):
-                nc.tensor.matmul(
-                    agg_ps[b][half][:], xT[b][:, t, :], adj_sb[:, t, half * W : (half + 1) * W],
-                    start=(t == 0), stop=(t == JB - 1),
-                )
-
-        for b in range(CB):
-            x = held.tile([P, N], F32, name=f"x{b}")
-            for t in range(JB):
-                nc.vector.tensor_tensor(
-                    x[:, t * P : (t + 1) * P],
-                    emb_sb[b][:].indirect(offsets[:, t * (P // 16) : (t + 1) * (P // 16)]),
-                    nf_sb[b][:, t * P : (t + 1) * P],
-                    MULT,
-                )
-                xT_ps = banks.tile([P, P], F32, name="xT_ps", tag="bank")
-                if b == 0:
-                    nc.tensor.matmul(xT_ps[:], x[:, t * P : (t + 1) * P], identity[:], start=True, stop=True)
-                else:
-                    nc.tensor.transpose(xT_ps[:], x[:, t * P : (t + 1) * P], identity[:])
-                nc.scalar.copy(xT[b][:, t, :], xT_ps[:])
-                if b == 1:
-                    sum_over_j(0, t)
-        for t in range(JB):
-            sum_over_j(1, t)
-
         agg = [held.tile([P, N], BF16, name=f"agg{b}") for b in range(CB)]
-        for b in range(CB):
-            nc.vector.tensor_copy(agg[b][:, 0:W], agg_ps[b][0][:])
-            nc.scalar.copy(agg[b][:, W:N], agg_ps[b][1][:])
+
+        def sum_over_j(b, half, t):
+            nc.tensor.matmul(
+                agg_ps[b][half][:], xT[b][:, t, :], adj_sb[:, t, half * W : (half + 1) * W],
+                start=(t == 0), stop=(t == JB - 1),
+            )
+
+        def round_agg(b, half):
+            if half == 0:
+                nc.vector.tensor_copy(agg[b][:, 0:W], agg_ps[b][0][:])
+            else:
+                nc.scalar.copy(agg[b][:, W:N], agg_ps[b][1][:])
 
         y = [held.tile([P, N], F32, name=f"y{k}") for k in range(HB)]
-        for half in range(HALVES):
+
+        def project(half):
             cols = slice(half * W, (half + 1) * W)
             out_ps = [banks.tile([P, W], F32, name=f"out_ps{half}_{k}", tag="bank") for k in range(HB)]
             for b in range(CB):
@@ -98,3 +97,20 @@ def tile_gcn_rec_kernel(tc, emb, nf, adj_t, w1, b1, offs, out):
                 else:
                     nc.vector.tensor_scalar(y[k][:, cols], out_ps[k][:], b1_sb[:, k : k + 1], 0.0, op0=ADD, op1=MAX)
                 nc.sync.dma_start(out[k * P : (k + 1) * P, cols], y[k][:, cols])
+
+        for t in range(JB):
+            gate_and_flip(0, t)
+        for t in range(JB):
+            gate_and_flip(1, t)
+            sum_over_j(0, 0, t)
+            sum_over_j(0, 1, t)
+        round_agg(0, 0)
+        round_agg(0, 1)
+        for t in range(JB):
+            sum_over_j(1, 0, t)
+        round_agg(1, 0)
+        project(0)
+        for t in range(JB):
+            sum_over_j(1, 1, t)
+        round_agg(1, 1)
+        project(1)

@@ -82,20 +82,28 @@ def tile_gcn_rec_kernel(tc, emb, nf, adj_t, w1, b1, offs, out):
 
         y = [held.tile([P, N], F32, name=f"y{k}") for k in range(HB)]
 
-        def project(half):
-            cols = slice(half * W, (half + 1) * W)
-            out_ps = [banks.tile([P, W], F32, name=f"out_ps{half}_{k}", tag="bank") for k in range(HB)]
-            for b in range(CB):
-                for k in range(HB):
-                    nc.tensor.matmul(
-                        out_ps[k][:], w1_sb[:, b, k * P : (k + 1) * P], agg[b][:, cols],
-                        start=(b == 0), stop=(b == CB - 1),
-                    )
+        out_ps = [[None] * HB for half in range(HALVES)]
+
+        def project(b, half, k):
+            nc.tensor.matmul(
+                out_ps[half][k][:], w1_sb[:, b, k * P : (k + 1) * P], agg[b][:, half * W : (half + 1) * W],
+                start=(b == 0), stop=(b == CB - 1),
+            )
+
+        def open_out(half):
             for k in range(HB):
+                out_ps[half][k] = banks.tile([P, W], F32, name=f"out_ps{half}_{k}", tag="bank")
+                project(0, half, k)
+
+        def close_out(half, blocks):
+            cols = slice(half * W, (half + 1) * W)
+            for k in blocks:
+                project(1, half, k)
+            for k in blocks:
                 if k % 2 == 0:
-                    nc.scalar.activation(y[k][:, cols], out_ps[k][:], RELU, bias=b1_sb[:, k : k + 1])
+                    nc.scalar.activation(y[k][:, cols], out_ps[half][k][:], RELU, bias=b1_sb[:, k : k + 1])
                 else:
-                    nc.vector.tensor_scalar(y[k][:, cols], out_ps[k][:], b1_sb[:, k : k + 1], 0.0, op0=ADD, op1=MAX)
+                    nc.vector.tensor_scalar(y[k][:, cols], out_ps[half][k][:], b1_sb[:, k : k + 1], 0.0, op0=ADD, op1=MAX)
                 nc.sync.dma_start(out[k * P : (k + 1) * P, cols], y[k][:, cols])
 
         for t in range(JB):
@@ -109,8 +117,11 @@ def tile_gcn_rec_kernel(tc, emb, nf, adj_t, w1, b1, offs, out):
         for t in range(JB):
             sum_over_j(1, 0, t)
         round_agg(1, 0)
-        project(0)
+        open_out(0)
+        close_out(0, range(0, HB // 2))
         for t in range(JB):
             sum_over_j(1, 1, t)
         round_agg(1, 1)
-        project(1)
+        close_out(0, range(HB // 2, HB))
+        open_out(1)
+        close_out(1, range(HB))

@@ -61,7 +61,10 @@ def tile_gcn_rec_kernel(tc, emb, nf, adj_t, w1, b1, offs, out):
                 nc.tensor.matmul(xT_ps[:], piece, identity[:], start=True, stop=True)
             else:
                 nc.tensor.transpose(xT_ps[:], piece, identity[:])
-            nc.scalar.copy(xT[b][:, t, :], xT_ps[:])
+            if b == CB - 1 and t == JB - 1:
+                nc.vector.tensor_copy(xT[b][:, t, :], xT_ps[:])
+            else:
+                nc.scalar.copy(xT[b][:, t, :], xT_ps[:])
 
         agg_ps = [
             [banks.tile([P, W], F32, name=f"agg_ps{b}_{half}", tag="bank") for half in range(HALVES)] for b in range(CB)
@@ -75,10 +78,11 @@ def tile_gcn_rec_kernel(tc, emb, nf, adj_t, w1, b1, offs, out):
             )
 
         def round_agg(b, half):
-            if half == 0:
-                nc.vector.tensor_copy(agg[b][:, 0:W], agg_ps[b][0][:])
+            cols = slice(half * W, (half + 1) * W)
+            if b == 0 and half == 1:
+                nc.scalar.copy(agg[b][:, cols], agg_ps[b][half][:])
             else:
-                nc.scalar.copy(agg[b][:, W:N], agg_ps[b][1][:])
+                nc.vector.tensor_copy(agg[b][:, cols], agg_ps[b][half][:])
 
         y = [held.tile([P, N], F32, name=f"y{k}") for k in range(HB)]
 

@@ -84,7 +84,8 @@ def tile_gcn_rec_kernel(tc, emb, nf, adj_t, w1, b1, offs, out):
             else:
                 nc.vector.tensor_copy(agg[b][:, cols], agg_ps[b][half][:])
 
-        y = [held.tile([P, N], F32, name=f"y{k}") for k in range(HB)]
+        y = [held.tile([P, HB, W], F32, name=f"y{half}") for half in range(HALVES)]
+        out_blocks = out.rearrange("(k p) i -> p k i", p=P)
 
         out_ps = [[None] * HB for half in range(HALVES)]
 
@@ -100,15 +101,16 @@ def tile_gcn_rec_kernel(tc, emb, nf, adj_t, w1, b1, offs, out):
                 project(0, half, k)
 
         def close_out(half, blocks):
-            cols = slice(half * W, (half + 1) * W)
             for k in blocks:
                 project(1, half, k)
             for k in blocks:
                 if k % 2 == 0:
-                    nc.scalar.activation(y[k][:, cols], out_ps[half][k][:], RELU, bias=b1_sb[:, k : k + 1])
+                    nc.scalar.activation(y[half][:, k, :], out_ps[half][k][:], RELU, bias=b1_sb[:, k : k + 1])
                 else:
-                    nc.vector.tensor_scalar(y[k][:, cols], out_ps[half][k][:], b1_sb[:, k : k + 1], 0.0, op0=ADD, op1=MAX)
-                nc.sync.dma_start(out[k * P : (k + 1) * P, cols], y[k][:, cols])
+                    nc.vector.tensor_scalar(y[half][:, k, :], out_ps[half][k][:], b1_sb[:, k : k + 1], 0.0, op0=ADD, op1=MAX)
+            nc.sync.dma_start(
+                out_blocks[:, blocks.start : blocks.stop, half * W : (half + 1) * W], y[half][:, blocks.start : blocks.stop, :]
+            )
 
         for t in range(JB):
             gate_and_flip(0, t)
@@ -128,4 +130,5 @@ def tile_gcn_rec_kernel(tc, emb, nf, adj_t, w1, b1, offs, out):
         round_agg(1, 1)
         close_out(0, range(HB // 2, HB))
         open_out(1)
-        close_out(1, range(HB))
+        close_out(1, range(0, HB // 2))
+        close_out(1, range(HB // 2, HB))

@@ -100,7 +100,10 @@ def tile_gcn_rec_kernel(tc, emb, nf, adj_t, w1, b1, offs, out):
                 out_ps[half][k] = banks.tile([P, W], F32, name=f"out_ps{half}_{k}", tag="bank")
                 project(0, half, k)
 
-        def close_out(half, blocks):
+        def store(half, first, last):
+            nc.sync.dma_start(out_blocks[:, first:last, half * W : (half + 1) * W], y[half][:, first:last, :])
+
+        def close_out(half, blocks, together):
             for k in blocks:
                 project(1, half, k)
             for k in blocks:
@@ -108,9 +111,10 @@ def tile_gcn_rec_kernel(tc, emb, nf, adj_t, w1, b1, offs, out):
                     nc.scalar.activation(y[half][:, k, :], out_ps[half][k][:], RELU, bias=b1_sb[:, k : k + 1])
                 else:
                     nc.vector.tensor_scalar(y[half][:, k, :], out_ps[half][k][:], b1_sb[:, k : k + 1], 0.0, op0=ADD, op1=MAX)
-            nc.sync.dma_start(
-                out_blocks[:, blocks.start : blocks.stop, half * W : (half + 1) * W], y[half][:, blocks.start : blocks.stop, :]
-            )
+                if not together:
+                    store(half, k, k + 1)
+            if together:
+                store(half, blocks.start, blocks.stop)
 
         for t in range(JB):
             gate_and_flip(0, t)
@@ -124,11 +128,11 @@ def tile_gcn_rec_kernel(tc, emb, nf, adj_t, w1, b1, offs, out):
             sum_over_j(1, 0, t)
         round_agg(1, 0)
         open_out(0)
-        close_out(0, range(0, HB // 2))
+        close_out(0, range(0, HB // 2), together=False)
         for t in range(JB):
             sum_over_j(1, 1, t)
         round_agg(1, 1)
-        close_out(0, range(HB // 2, HB))
+        close_out(0, range(HB // 2, HB), together=True)
         open_out(1)
-        close_out(1, range(0, HB // 2))
-        close_out(1, range(HB // 2, HB))
+        close_out(1, range(0, HB // 2), together=True)
+        close_out(1, range(HB // 2, HB), together=True)

@@ -6,9 +6,9 @@ C, S, N, HID = 256, 2048, 512, 512
 CB, JB, HB = C // P, N // P, HID // P
 GB = 2
 G = N // GB
-TG = JB // GB
 HALVES = 2
 W = N // HALVES
+WARM = 2
 FLOPS = 2 * C * N * N + 2 * C * N * HID
 
 F32, BF16, U16 = mybir.dt.float32, mybir.dt.bfloat16, mybir.dt.uint16
@@ -32,12 +32,18 @@ def tile_gcn_rec_kernel(tc, emb, nf, adj_t, w1, b1, offs, out):
         nc.sync.dma_start(emb_sb[0][:], emb[0:P, :])
         nc.sync.dma_start(nf_sb[0][:], nf[0:P, :])
         nc.sync.dma_start(emb_sb[1][:], emb[P : 2 * P, :])
-        for g in range(GB):
+
+        def load_nf1(g):
             nc.sync.dma_start(nf_sb[1][:, g * G : (g + 1) * G], nf[P : 2 * P, g * G : (g + 1) * G])
-        for g in range(GB):
-            nc.sync.dma_start(
-                adj_sb[:, g * TG : (g + 1) * TG, :], adj_t[g * G : (g + 1) * G, :].rearrange("(t p) i -> p t i", p=P)
-            )
+
+        def load_adj(t):
+            nc.sync.dma_start(adj_sb[:, t, :], adj_t[t * P : (t + 1) * P, :])
+
+        load_nf1(0)
+        load_adj(0)
+        load_nf1(1)
+        for t in range(1, JB):
+            load_adj(t)
         nc.sync.dma_start(w1_sb[:], w1.rearrange("(b p) h -> p b h", p=P))
         with nc.allow_non_contiguous_dma(reason="512 bias values, one to a partition"):
             nc.sync.dma_start(b1_sb[:], b1.rearrange("(k p) o -> p (k o)", p=P))
@@ -57,7 +63,7 @@ def tile_gcn_rec_kernel(tc, emb, nf, adj_t, w1, b1, offs, out):
                 MULT,
             )
             xT_ps = banks.tile([P, P], F32, name="xT_ps", tag="bank")
-            if b == 0:
+            if b == 0 and t < WARM:
                 nc.tensor.matmul(xT_ps[:], piece, identity[:], start=True, stop=True)
             else:
                 nc.tensor.transpose(xT_ps[:], piece, identity[:])
@@ -79,7 +85,7 @@ def tile_gcn_rec_kernel(tc, emb, nf, adj_t, w1, b1, offs, out):
 
         def round_agg(b, half):
             cols = slice(half * W, (half + 1) * W)
-            if b == 0 and half == 1:
+            if half == 1:
                 nc.scalar.copy(agg[b][:, cols], agg_ps[b][half][:])
             else:
                 nc.vector.tensor_copy(agg[b][:, cols], agg_ps[b][half][:])
@@ -119,19 +125,20 @@ def tile_gcn_rec_kernel(tc, emb, nf, adj_t, w1, b1, offs, out):
         for t in range(JB):
             gate_and_flip(0, t)
         for t in range(JB):
-            gate_and_flip(1, t)
             sum_over_j(0, 0, t)
             sum_over_j(0, 1, t)
+            gate_and_flip(1, t)
         round_agg(0, 0)
         round_agg(0, 1)
         for t in range(JB):
             sum_over_j(1, 0, t)
+            if t > 0:
+                sum_over_j(1, 1, t - 1)
         round_agg(1, 0)
+        sum_over_j(1, 1, JB - 1)
+        round_agg(1, 1)
         open_out(0)
         close_out(0, range(0, HB // 2), together=False)
-        for t in range(JB):
-            sum_over_j(1, 1, t)
-        round_agg(1, 1)
         close_out(0, range(HB // 2, HB), together=True)
         open_out(1)
         close_out(1, range(0, HB // 2), together=True)

@@ -90,7 +90,7 @@ def tile_gcn_rec_kernel(tc, emb, nf, adj_t, w1, b1, offs, out):
             else:
                 nc.vector.tensor_copy(agg[b][:, cols], agg_ps[b][half][:])
 
-        y = [held.tile([P, HB, W], F32, name=f"y{half}") for half in range(HALVES)]
+        y = held.tile([P, HB, N], F32, name="y")
         out_blocks = out.rearrange("(k p) i -> p k i", p=P)
 
         out_ps = [[None] * HB for half in range(HALVES)]
@@ -101,26 +101,15 @@ def tile_gcn_rec_kernel(tc, emb, nf, adj_t, w1, b1, offs, out):
                 start=(b == 0), stop=(b == CB - 1),
             )
 
-        def open_out(half):
-            for k in range(HB):
-                out_ps[half][k] = banks.tile([P, W], F32, name=f"out_ps{half}_{k}", tag="bank")
-                project(0, half, k)
+        def bias_and_relu(half, k):
+            cols = slice(half * W, (half + 1) * W)
+            if half == 0:
+                nc.scalar.activation(y[:, k, cols], out_ps[half][k][:], RELU, bias=b1_sb[:, k : k + 1])
+            else:
+                nc.vector.tensor_scalar(y[:, k, cols], out_ps[half][k][:], b1_sb[:, k : k + 1], 0.0, op0=ADD, op1=MAX)
 
-        def store(half, first, last):
-            nc.sync.dma_start(out_blocks[:, first:last, half * W : (half + 1) * W], y[half][:, first:last, :])
-
-        def close_out(half, blocks, together):
-            for k in blocks:
-                project(1, half, k)
-            for k in blocks:
-                if k % 2 == 0:
-                    nc.scalar.activation(y[half][:, k, :], out_ps[half][k][:], RELU, bias=b1_sb[:, k : k + 1])
-                else:
-                    nc.vector.tensor_scalar(y[half][:, k, :], out_ps[half][k][:], b1_sb[:, k : k + 1], 0.0, op0=ADD, op1=MAX)
-                if not together:
-                    store(half, k, k + 1)
-            if together:
-                store(half, blocks.start, blocks.stop)
+        def store(first, last, cols):
+            nc.sync.dma_start(out_blocks[:, first:last, cols], y[:, first:last, cols])
 
         for t in range(JB):
             gate_and_flip(0, t)
@@ -137,9 +126,21 @@ def tile_gcn_rec_kernel(tc, emb, nf, adj_t, w1, b1, offs, out):
         round_agg(1, 0)
         sum_over_j(1, 1, JB - 1)
         round_agg(1, 1)
-        open_out(0)
-        close_out(0, range(0, HB // 2), together=False)
-        close_out(0, range(HB // 2, HB), together=True)
-        open_out(1)
-        close_out(1, range(0, HB // 2), together=True)
-        close_out(1, range(HB // 2, HB), together=True)
+        for k in range(HB):
+            out_ps[0][k] = banks.tile([P, W], F32, name=f"out_ps0_{k}", tag="bank")
+            project(0, 0, k)
+        for k in range(HB):
+            project(1, 0, k)
+            bias_and_relu(0, k)
+            if k == 0:
+                store(0, 1, slice(0, W))
+            out_ps[1][k] = banks.tile([P, W], F32, name=f"out_ps1_{k}", tag="bank")
+            project(0, 1, k)
+            project(1, 1, k)
+            bias_and_relu(1, k)
+            if k == 0:
+                store(0, 1, slice(W, N))
+            if k == 1:
+                store(1, 2, slice(0, N))
+            if k == HB - 1:
+                store(2, HB, slice(0, N))

@@ -45,8 +45,7 @@ def tile_gcn_rec_kernel(tc, emb, nf, adj_t, w1, b1, offs, out):
         for t in range(1, JB):
             load_adj(t)
         nc.sync.dma_start(w1_sb[:], w1.rearrange("(b p) h -> p b h", p=P))
-        with nc.allow_non_contiguous_dma(reason="512 bias values, one to a partition"):
-            nc.sync.dma_start(b1_sb[:], b1.rearrange("(k p) o -> p (k o)", p=P))
+        nc.sync.dma_start(b1_sb[:], b1.rearrange("(p k) o -> p (k o)", k=HB))
 
         identity = held.tile([P, P], F32, name="identity")
         make_identity(nc, identity[:])
@@ -91,13 +90,13 @@ def tile_gcn_rec_kernel(tc, emb, nf, adj_t, w1, b1, offs, out):
                 nc.vector.tensor_copy(agg[b][:, cols], agg_ps[b][half][:])
 
         y = held.tile([P, HB, N], F32, name="y")
-        out_blocks = out.rearrange("(k p) i -> p k i", p=P)
+        out_blocks = out.rearrange("(p k) i -> p k i", k=HB)
 
         out_ps = [[None] * HB for half in range(HALVES)]
 
         def project(b, half, k):
             nc.tensor.matmul(
-                out_ps[half][k][:], w1_sb[:, b, k * P : (k + 1) * P], agg[b][:, half * W : (half + 1) * W],
+                out_ps[half][k][:], w1_sb[:, b, k:HID:HB], agg[b][:, half * W : (half + 1) * W],
                 start=(b == 0), stop=(b == CB - 1),
             )
 

@@ -4,8 +4,7 @@ from concourse.masks import make_identity
 P = 128
 C, S, N, HID = 256, 2048, 512, 512
 CB, JB, HB = C // P, N // P, HID // P
-GB = 2
-G = N // GB
+G = N // 2
 HALVES = 2
 W = N // HALVES
 WARM = 2
@@ -25,26 +24,24 @@ def tile_gcn_rec_kernel(tc, emb, nf, adj_t, w1, b1, offs, out):
         offsets = held.tile([P, N // 16], U16, name="offsets")
         nc.sync.dma_start(offsets[:], offs)
         emb_sb = [held.tile([P, S], F32, name=f"emb{b}") for b in range(CB)]
-        nf_sb = [held.tile([P, N], F32, name=f"nf{b}") for b in range(CB)]
+        nf_sb = held.tile([P, CB * N], F32, name="nf_sb")
         adj_sb = held.tile([P, JB, N], BF16, name="adj_sb")
         w1_sb = held.tile([P, CB, HID], BF16, name="w1_sb")
         b1_sb = held.tile([P, HB], F32, name="b1_sb")
-        nc.sync.dma_start(emb_sb[0][:], emb[0:P, :])
-        nc.sync.dma_start(nf_sb[0][:], nf[0:P, :])
-        nc.sync.dma_start(emb_sb[1][:], emb[P : 2 * P, :])
-
-        def load_nf1(g):
-            nc.sync.dma_start(nf_sb[1][:, g * G : (g + 1) * G], nf[P : 2 * P, g * G : (g + 1) * G])
+        emb_blocks = emb.rearrange("(p b) s -> b p s", b=CB)
+        nf_rows = nf.rearrange("(p b) j -> p (b j)", b=CB)
 
         def load_adj(t):
             nc.sync.dma_start(adj_sb[:, t, :], adj_t[t * P : (t + 1) * P, :])
 
-        load_nf1(0)
+        nc.sync.dma_start(emb_sb[0][:], emb_blocks[0])
+        nc.sync.dma_start(nf_sb[:, 0 : N + G], nf_rows[:, 0 : N + G])
+        nc.sync.dma_start(emb_sb[1][:], emb_blocks[1])
         load_adj(0)
-        load_nf1(1)
+        nc.sync.dma_start(nf_sb[:, N + G : CB * N], nf_rows[:, N + G : CB * N])
         for t in range(1, JB):
             load_adj(t)
-        nc.sync.dma_start(w1_sb[:], w1.rearrange("(b p) h -> p b h", p=P))
+        nc.sync.dma_start(w1_sb[:], w1.rearrange("(p b) h -> p b h", b=CB))
         nc.sync.dma_start(b1_sb[:], b1.rearrange("(p k) o -> p (k o)", k=HB))
 
         identity = held.tile([P, P], F32, name="identity")
@@ -58,7 +55,7 @@ def tile_gcn_rec_kernel(tc, emb, nf, adj_t, w1, b1, offs, out):
             nc.vector.tensor_tensor(
                 piece,
                 emb_sb[b][:].indirect(offsets[:, t * (P // 16) : (t + 1) * (P // 16)]),
-                nf_sb[b][:, t * P : (t + 1) * P],
+                nf_sb[:, b * N + t * P : b * N + (t + 1) * P],
                 MULT,
             )
             xT_ps = banks.tile([P, P], F32, name="xT_ps", tag="bank")

@@ -35,8 +35,9 @@ def tile_gcn_rec_kernel(tc, emb, nf, adj_t, w1, b1, offs, out):
             nc.sync.dma_start(adj_sb[:, t, :], adj_t[t * P : (t + 1) * P, :])
 
         nc.sync.dma_start(emb_sb[0][:], emb_blocks[0])
-        nc.sync.dma_start(nf_sb[:, 0 : N + G], nf_rows[:, 0 : N + G])
+        nc.sync.dma_start(nf_sb[:, 0:N], nf_rows[:, 0:N])
         nc.sync.dma_start(emb_sb[1][:], emb_blocks[1])
+        nc.sync.dma_start(nf_sb[:, N : N + G], nf_rows[:, N : N + G])
         load_adj(0)
         nc.sync.dma_start(nf_sb[:, N + G : CB * N], nf_rows[:, N + G : CB * N])
         for t in range(1, JB):

import concourse.mybir as mybir
from concourse.masks import make_identity

P = 128
C, S, N, HID = 256, 2048, 512, 512
CB, JB, HB = C // P, N // P, HID // P
G = N // 2
HALVES = 2
W = N // HALVES
WARM = 2
FLOPS = 2 * C * N * N + 2 * C * N * HID

F32, BF16, U16 = mybir.dt.float32, mybir.dt.bfloat16, mybir.dt.uint16
MULT, ADD, MAX = mybir.AluOpType.mult, mybir.AluOpType.add, mybir.AluOpType.max
RELU = mybir.ActivationFunctionType.Relu


def tile_gcn_rec_kernel(tc, emb, nf, adj_t, w1, b1, offs, out):
    nc = tc.nc
    with (
        tc.tile_pool(name="held", bufs=1) as held,
        tc.psum_pool(name="banks", bufs=8) as banks,
    ):
        offsets = held.tile([P, N // 16], U16, name="offsets")
        nc.sync.dma_start(offsets[:], offs)
        emb_sb = [held.tile([P, S], F32, name=f"emb{b}") for b in range(CB)]
        nf_sb = held.tile([P, CB * N], F32, name="nf_sb")
        adj_sb = held.tile([P, JB, N], BF16, name="adj_sb")
        w1_sb = held.tile([P, CB, HID], BF16, name="w1_sb")
        b1_sb = held.tile([P, HB], F32, name="b1_sb")
        emb_blocks = emb.rearrange("(p b) s -> b p s", b=CB)
        nf_rows = nf.rearrange("(p b) j -> p (b j)", b=CB)

        def load_adj(t):
            nc.sync.dma_start(adj_sb[:, t, :], adj_t[t * P : (t + 1) * P, :])

        nc.sync.dma_start(emb_sb[0][:], emb_blocks[0])
        nc.sync.dma_start(nf_sb[:, 0:N], nf_rows[:, 0:N])
        nc.sync.dma_start(emb_sb[1][:], emb_blocks[1])
        nc.sync.dma_start(nf_sb[:, N : N + G], nf_rows[:, N : N + G])
        load_adj(0)
        nc.sync.dma_start(nf_sb[:, N + G : CB * N], nf_rows[:, N + G : CB * N])
        for t in range(1, JB):
            load_adj(t)
        nc.sync.dma_start(w1_sb[:], w1.rearrange("(p b) h -> p b h", b=CB))
        nc.sync.dma_start(b1_sb[:], b1.rearrange("(p k) o -> p (k o)", k=HB))

        identity = held.tile([P, P], F32, name="identity")
        make_identity(nc, identity[:])

        x = [held.tile([P, N], F32, name=f"x{b}") for b in range(CB)]
        xT = [held.tile([P, JB, P], BF16, name=f"xT{b}") for b in range(CB)]

        def gate_and_flip(b, t):
            piece = x[b][:, t * P : (t + 1) * P]
            nc.vector.tensor_tensor(
                piece,
                emb_sb[b][:].indirect(offsets[:, t * (P // 16) : (t + 1) * (P // 16)]),
                nf_sb[:, b * N + t * P : b * N + (t + 1) * P],
                MULT,
            )
            xT_ps = banks.tile([P, P], F32, name="xT_ps", tag="bank")
            if b == 0 and t < WARM:
                nc.tensor.matmul(xT_ps[:], piece, identity[:], start=True, stop=True)
            else:
                nc.tensor.transpose(xT_ps[:], piece, identity[:])
            if b == CB - 1 and t == JB - 1:
                nc.vector.tensor_copy(xT[b][:, t, :], xT_ps[:])
            else:
                nc.scalar.copy(xT[b][:, t, :], xT_ps[:])

        agg_ps = [
            [banks.tile([P, W], F32, name=f"agg_ps{b}_{half}", tag="bank") for half in range(HALVES)] for b in range(CB)
        ]
        agg = [held.tile([P, N], BF16, name=f"agg{b}") for b in range(CB)]

        def sum_over_j(b, half, t):
            nc.tensor.matmul(
                agg_ps[b][half][:], xT[b][:, t, :], adj_sb[:, t, half * W : (half + 1) * W],
                start=(t == 0), stop=(t == JB - 1),
            )

        def round_agg(b, half):
            cols = slice(half * W, (half + 1) * W)
            if half == 1:
                nc.scalar.copy(agg[b][:, cols], agg_ps[b][half][:])
            else:
                nc.vector.tensor_copy(agg[b][:, cols], agg_ps[b][half][:])

        y = held.tile([P, HB, N], F32, name="y")
        out_blocks = out.rearrange("(p k) i -> p k i", k=HB)

        out_ps = [[None] * HB for half in range(HALVES)]

        def project(b, half, k):
            nc.tensor.matmul(
                out_ps[half][k][:], w1_sb[:, b, k:HID:HB], agg[b][:, half * W : (half + 1) * W],
                start=(b == 0), stop=(b == CB - 1),
            )

        def bias_and_relu(half, k):
            cols = slice(half * W, (half + 1) * W)
            if half == 0:
                nc.scalar.activation(y[:, k, cols], out_ps[half][k][:], RELU, bias=b1_sb[:, k : k + 1])
            else:
                nc.vector.tensor_scalar(y[:, k, cols], out_ps[half][k][:], b1_sb[:, k : k + 1], 0.0, op0=ADD, op1=MAX)

        def store(first, last, cols):
            nc.sync.dma_start(out_blocks[:, first:last, cols], y[:, first:last, cols])

        for t in range(JB):
            gate_and_flip(0, t)
        for t in range(JB):
            sum_over_j(0, 0, t)
            sum_over_j(0, 1, t)
            gate_and_flip(1, t)
        round_agg(0, 0)
        round_agg(0, 1)
        for t in range(JB):
            sum_over_j(1, 0, t)
            if t > 0:
                sum_over_j(1, 1, t - 1)
        round_agg(1, 0)
        sum_over_j(1, 1, JB - 1)
        round_agg(1, 1)
        for k in range(HB):
            out_ps[0][k] = banks.tile([P, W], F32, name=f"out_ps0_{k}", tag="bank")
            project(0, 0, k)
        for k in range(HB):
            project(1, 0, k)
            bias_and_relu(0, k)
            if k == 0:
                store(0, 1, slice(0, W))
            out_ps[1][k] = banks.tile([P, W], F32, name=f"out_ps1_{k}", tag="bank")
            project(0, 1, k)
            project(1, 1, k)
            bias_and_relu(1, k)
            if k == 0:
                store(0, 1, slice(W, N))
            if k == 1:
                store(1, 2, slice(0, N))
            if k == HB - 1:
                store(2, HB, slice(0, N))
